import numpy as np
import ml_dtypes

BF16 = ml_dtypes.bfloat16


def bf(x):
    return np.asarray(x, np.float32).astype(BF16)


def f32(x):
    return np.asarray(x, np.float32)


def f64(x):
    return np.asarray(x).astype(np.float64)


def striped(idx):
    return np.tile(idx.reshape(-1, 16).T, (8, 1))


S, D, M, DEG, NB, PER, N = 1024, 128, 512, 2, 3, 2, 2048


def setup_inputs():
    return {
        "table": bf(np.random.standard_normal((S, D))),
        "w_self0": bf(np.random.standard_normal((D, M)) / np.sqrt(D)),
        "w_neigh0": bf(np.random.standard_normal((D, M)) / np.sqrt(D * DEG)),
        "b0": f32(0.1 * np.random.standard_normal((M, 1))),
        "w_hid": f32(np.random.standard_normal((NB * PER, M, M)) * np.sqrt(2.0 / M)),
        "b_hid": f32(0.1 * np.random.standard_normal((M, NB * PER))),
        "offs": striped(np.random.permutation(np.tile(np.arange(S), 2))[:N]),
    }


def reference(table, w_self0, w_neigh0, b0, w_hid, b_hid, offs):
    idx = offs[:16].T.reshape(-1)
    t = f64(table)
    agg = t[idx].reshape(DEG, S, D).sum(axis=0)
    x = np.maximum(f64(w_self0).T @ t.T + f64(w_neigh0).T @ agg.T + f64(b0), 0.0)
    w, b = f64(w_hid), f64(b_hid)
    for i in range(NB):
        temp = x
        for u in range(PER):
            l = i * PER + u
            x = np.maximum(w[l].T @ x + b[:, l:l + 1], 0.0)
        x = 0.5 * (temp + x)
    return x

@@ -1,0 +1,149 @@
+import concourse.mybir as mybir
+from concourse.masks import make_identity
+
+BF16, F32, U16 = mybir.dt.bfloat16, mybir.dt.float32, mybir.dt.uint16
+RELU = mybir.ActivationFunctionType.Relu
+ADD, MAX, MULT = mybir.AluOpType.add, mybir.AluOpType.max, mybir.AluOpType.mult
+
+P = 128
+NODES = 1024
+D_IN = 128
+D_HID = 512
+DEGREE = 2
+LAYERS = 6
+HALF = 512
+N_HALVES = NODES // HALF
+N_BLOCKS = D_HID // P
+PIECE_COLS = HALF // 16
+
+FLOPS = 2 * NODES * D_HID * (2 * D_IN + LAYERS * D_HID)
+
+
+def tile_gresnet_b_kernel(tc, table, w_self0, w_neigh0, b0, w_hid, b_hid, offs, out):
+    nc = tc.nc
+    with (
+        tc.tile_pool(name="held", bufs=1) as held,
+        tc.tile_pool(name="operands", bufs=2 * N_BLOCKS * N_HALVES) as operands,
+        tc.tile_pool(name="residuals", bufs=2 * N_BLOCKS * N_HALVES) as residuals,
+        tc.tile_pool(name="passing", bufs=4) as passing,
+        tc.psum_pool(name="banks", bufs=8) as banks,
+    ):
+        offsets = held.tile([P, DEGREE * NODES // 16], U16, name="offsets")
+        nc.sync.dma_start(offsets[:], offs)
+        table_rows = held.tile([P, NODES // P, D_IN], BF16, name="table_rows")
+        nc.sync.dma_start(table_rows[:], table.rearrange("(a p) k -> p a k", p=P))
+        w_f32 = []
+        for l in range(LAYERS):
+            w_f32.append(held.tile([P, N_BLOCKS, D_HID], F32, name=f"w_f32_{l}"))
+            nc.sync.dma_start(w_f32[l][:], w_hid[l].rearrange("(a p) m -> p a m", p=P))
+
+        w_self = held.tile([D_IN, D_HID], BF16, name="w_self")
+        nc.scalar.dma_start(w_self[:], w_self0)
+        w_neigh = held.tile([D_IN, D_HID], BF16, name="w_neigh")
+        nc.scalar.dma_start(w_neigh[:], w_neigh0)
+        bias_first = held.tile([P, N_BLOCKS], F32, name="bias_first")
+        with nc.allow_non_contiguous_dma(reason="512 biases, one value to a partition and block"):
+            nc.scalar.dma_start(bias_first[:], b0.rearrange("(a p) o -> p (a o)", p=P))
+        bias_hid = held.tile([P, N_BLOCKS, LAYERS], F32, name="bias_hid")
+        nc.scalar.dma_start(bias_hid[:], b_hid.rearrange("(a p) l -> p a l", p=P))
+        bias_halved = held.tile([P, N_BLOCKS, LAYERS], F32, name="bias_halved")
+        nc.vector.tensor_scalar(bias_halved[:], bias_hid[:], 0.5, None, MULT)
+
+        w_bf16 = [held.tile([P, N_BLOCKS, D_HID], BF16, name=f"w_bf16_{l}") for l in range(LAYERS)]
+
+        def round_weights(l):
+            for kb in range(N_BLOCKS):
+                nc.vector.tensor_copy(w_bf16[l][:, kb, :], w_f32[l][:, kb, :])
+
+        identity = held.tile([P, P], BF16, name="identity")
+        make_identity(nc, identity[:])
+        table_t = held.tile([D_IN, NODES], BF16, name="table_t")
+        for h in range(N_HALVES):
+            flipped = banks.tile([D_IN, HALF], BF16, tag="bank", name="flipped")
+            for j in range(HALF // P):
+                a = h * (HALF // P) + j
+                nc.tensor.transpose(flipped[:, j * P:(j + 1) * P], table_rows[:, a, :], identity[:])
+            if h == 0:
+                nc.vector.tensor_copy(table_t[:, h * HALF:(h + 1) * HALF], flipped[:])
+            else:
+                nc.scalar.copy(table_t[:, h * HALF:(h + 1) * HALF], flipped[:])
+
+        round_weights(0)
+
+        acc_first = {}
+        for h in range(N_HALVES):
+            for mb in range(N_BLOCKS):
+                acc_first[mb, h] = banks.tile([P, HALF], F32, tag="bank", name=f"acc_first_{mb}_{h}")
+                nc.tensor.matmul(
+                    acc_first[mb, h][:],
+                    w_self[:, mb * P:(mb + 1) * P],
+                    table_t[:, h * HALF:(h + 1) * HALF],
+                    start=True,
+                    stop=False,
+                )
+        x_f32, x_bf16 = {}, {}
+        for h in range(N_HALVES):
+            for mb in range(N_BLOCKS):
+                for e in range(DEGREE):
+                    piece = e * N_HALVES + h
+                    neighbours = table_t[:].indirect(
+                        offsets[:, piece * PIECE_COLS:(piece + 1) * PIECE_COLS]
+                    )
+                    nc.tensor.matmul(
+                        acc_first[mb, h][:],
+                        w_neigh[:, mb * P:(mb + 1) * P],
+                        neighbours,
+                        start=False,
+                        stop=(e == DEGREE - 1),
+                    )
+                x_f32[mb, h] = residuals.tile([P, HALF], F32, tag="x_f32", name=f"x_f32_{mb}_{h}")
+                nc.scalar.activation(
+                    x_f32[mb, h][:], acc_first[mb, h][:], RELU, bias=bias_first[:, mb:mb + 1]
+                )
+                x_bf16[mb, h] = operands.tile([P, HALF], BF16, tag="x_bf16", name=f"x_bf16_{mb}_{h}")
+                nc.vector.tensor_copy(x_bf16[mb, h][:], x_f32[mb, h][:])
+
+        for l in range(LAYERS):
+            closes_block = l % 2 == 1
+            if l + 1 < LAYERS:
+                round_weights(l + 1)
+            y_bf16 = {}
+            for h in range(N_HALVES):
+                for mb in range(N_BLOCKS):
+                    acc = banks.tile([P, HALF], F32, tag="bank", name="acc")
+                    for kb in range(N_BLOCKS):
+                        nc.tensor.matmul(
+                            acc[:],
+                            w_bf16[l][:, kb, mb * P:(mb + 1) * P],
+                            x_bf16[kb, h][:],
+                            start=(kb == 0),
+                            stop=(kb == N_BLOCKS - 1),
+                        )
+                    if l + 1 < LAYERS:
+                        y_bf16[mb, h] = operands.tile([P, HALF], BF16, tag="x_bf16", name=f"y_bf16_{mb}_{h}")
+                    if not closes_block:
+                        if mb % 2 == 0:
+                            nc.scalar.activation(
+                                y_bf16[mb, h][:], acc[:], RELU, bias=bias_hid[:, mb, l:l + 1]
+                            )
+                        else:
+                            nc.vector.tensor_scalar(
+                                y_bf16[mb, h][:], acc[:], bias_hid[:, mb, l:l + 1], 0.0, ADD, MAX
+                            )
+                    else:
+                        half_relu = passing.tile([P, HALF], F32, tag="half_relu", name="half_relu")
+                        nc.scalar.activation(
+                            half_relu[:], acc[:], RELU, bias=bias_halved[:, mb, l:l + 1], scale=0.5
+                        )
+                        t = x_f32[mb, h]
+                        x_f32[mb, h] = residuals.tile([P, HALF], F32, tag="x_f32", name=f"x_f32_{mb}_{h}")
+                        nc.vector.scalar_tensor_tensor(
+                            x_f32[mb, h][:], t[:], 0.5, half_relu[:], MULT, ADD
+                        )
+                        if l + 1 < LAYERS:
+                            nc.vector.tensor_copy(y_bf16[mb, h][:], x_f32[mb, h][:])
+                        else:
+                            nc.sync.dma_start(
+                                out[mb * P:(mb + 1) * P, h * HALF:(h + 1) * HALF], x_f32[mb, h][:]
+                            )
+            x_bf16 = y_bf16

@@ -15,6 +15,7 @@ HALF = 512
 N_HALVES = NODES // HALF
 N_BLOCKS = D_HID // P
 PIECE_COLS = HALF // 16
+ROW_BLOCKS = HALF // P
 
 FLOPS = 2 * NODES * D_HID * (2 * D_IN + LAYERS * D_HID)
 
@@ -28,26 +29,26 @@ def tile_gresnet_b_kernel(tc, table, w_self0, w_neigh0, b0, w_hid, b_hid, offs, 
         tc.tile_pool(name="passing", bufs=4) as passing,
         tc.psum_pool(name="banks", bufs=8) as banks,
     ):
+        table_rows = held.tile([P, NODES // P, D_IN], BF16, name="table_rows")
+        table_blocks = table.rearrange("(a p) k -> p a k", p=P)
+        for h in range(N_HALVES):
+            blocks_of_half = slice(h * ROW_BLOCKS, (h + 1) * ROW_BLOCKS)
+            nc.sync.dma_start(table_rows[:, blocks_of_half, :], table_blocks[:, blocks_of_half, :])
+        w_self = held.tile([D_IN, D_HID], BF16, name="w_self")
+        nc.sync.dma_start(w_self[:], w_self0)
+        w_neigh = held.tile([D_IN, D_HID], BF16, name="w_neigh")
+        nc.sync.dma_start(w_neigh[:], w_neigh0)
         offsets = held.tile([P, DEGREE * NODES // 16], U16, name="offsets")
         nc.sync.dma_start(offsets[:], offs)
-        table_rows = held.tile([P, NODES // P, D_IN], BF16, name="table_rows")
-        nc.sync.dma_start(table_rows[:], table.rearrange("(a p) k -> p a k", p=P))
-        w_f32 = []
-        for l in range(LAYERS):
-            w_f32.append(held.tile([P, N_BLOCKS, D_HID], F32, name=f"w_f32_{l}"))
-            nc.sync.dma_start(w_f32[l][:], w_hid[l].rearrange("(a p) m -> p a m", p=P))
-
-        w_self = held.tile([D_IN, D_HID], BF16, name="w_self")
-        nc.scalar.dma_start(w_self[:], w_self0)
-        w_neigh = held.tile([D_IN, D_HID], BF16, name="w_neigh")
-        nc.scalar.dma_start(w_neigh[:], w_neigh0)
         bias_first = held.tile([P, N_BLOCKS], F32, name="bias_first")
         with nc.allow_non_contiguous_dma(reason="512 biases, one value to a partition and block"):
-            nc.scalar.dma_start(bias_first[:], b0.rearrange("(a p) o -> p (a o)", p=P))
+            nc.sync.dma_start(bias_first[:], b0.rearrange("(a p) o -> p (a o)", p=P))
+        w_f32 = [held.tile([P, N_BLOCKS, D_HID], F32, name=f"w_f32_{l}") for l in range(LAYERS)]
         bias_hid = held.tile([P, N_BLOCKS, LAYERS], F32, name="bias_hid")
-        nc.scalar.dma_start(bias_hid[:], b_hid.rearrange("(a p) l -> p a l", p=P))
-        bias_halved = held.tile([P, N_BLOCKS, LAYERS], F32, name="bias_halved")
-        nc.vector.tensor_scalar(bias_halved[:], bias_hid[:], 0.5, None, MULT)
+        for l in range(LAYERS):
+            nc.sync.dma_start(w_f32[l][:], w_hid[l].rearrange("(a p) m -> p a m", p=P))
+            if l == 0:
+                nc.sync.dma_start(bias_hid[:], b_hid.rearrange("(a p) l -> p a l", p=P))
 
         w_bf16 = [held.tile([P, N_BLOCKS, D_HID], BF16, name=f"w_bf16_{l}") for l in range(LAYERS)]
 
@@ -60,13 +61,10 @@ def tile_gresnet_b_kernel(tc, table, w_self0, w_neigh0, b0, w_hid, b_hid, offs, 
         table_t = held.tile([D_IN, NODES], BF16, name="table_t")
         for h in range(N_HALVES):
             flipped = banks.tile([D_IN, HALF], BF16, tag="bank", name="flipped")
-            for j in range(HALF // P):
-                a = h * (HALF // P) + j
+            for j in range(ROW_BLOCKS):
+                a = h * ROW_BLOCKS + j
                 nc.tensor.transpose(flipped[:, j * P:(j + 1) * P], table_rows[:, a, :], identity[:])
-            if h == 0:
-                nc.vector.tensor_copy(table_t[:, h * HALF:(h + 1) * HALF], flipped[:])
-            else:
-                nc.scalar.copy(table_t[:, h * HALF:(h + 1) * HALF], flipped[:])
+            nc.scalar.copy(table_t[:, h * HALF:(h + 1) * HALF], flipped[:])
 
         round_weights(0)
 
@@ -103,6 +101,8 @@ def tile_gresnet_b_kernel(tc, table, w_self0, w_neigh0, b0, w_hid, b_hid, offs, 
                 x_bf16[mb, h] = operands.tile([P, HALF], BF16, tag="x_bf16", name=f"x_bf16_{mb}_{h}")
                 nc.vector.tensor_copy(x_bf16[mb, h][:], x_f32[mb, h][:])
 
+        bias_halved = held.tile([P, N_BLOCKS, LAYERS], F32, name="bias_halved")
+        nc.vector.tensor_scalar(bias_halved[:], bias_hid[:], 0.5, None, MULT)
         for l in range(LAYERS):
             closes_block = l % 2 == 1
             if l + 1 < LAYERS:

@@ -2,7 +2,7 @@ import concourse.mybir as mybir
 from concourse.masks import make_identity
 
 BF16, F32, U16 = mybir.dt.bfloat16, mybir.dt.float32, mybir.dt.uint16
-RELU = mybir.ActivationFunctionType.Relu
+RELU, IDENTITY = mybir.ActivationFunctionType.Relu, mybir.ActivationFunctionType.Identity
 ADD, MAX, MULT = mybir.AluOpType.add, mybir.AluOpType.max, mybir.AluOpType.mult
 
 P = 128
@@ -16,8 +16,21 @@ N_HALVES = NODES // HALF
 N_BLOCKS = D_HID // P
 PIECE_COLS = HALF // 16
 ROW_BLOCKS = HALF // P
+NARROWEST = 128
 
 FLOPS = 2 * NODES * D_HID * (2 * D_IN + LAYERS * D_HID)
+
+
+def runs_of_nodes(l):
+    if l + 1 < LAYERS:
+        return [(h * HALF, HALF) for h in range(N_HALVES)]
+    runs, first = [(0, HALF)], HALF
+    while NODES - first > NARROWEST:
+        width = (NODES - first) // 2
+        runs.append((first, width))
+        first += width
+    runs.append((first, NODES - first))
+    return runs
 
 
 def tile_gresnet_b_kernel(tc, table, w_self0, w_neigh0, b0, w_hid, b_hid, offs, out):
@@ -25,8 +38,8 @@ def tile_gresnet_b_kernel(tc, table, w_self0, w_neigh0, b0, w_hid, b_hid, offs, 
     with (
         tc.tile_pool(name="held", bufs=1) as held,
         tc.tile_pool(name="operands", bufs=2 * N_BLOCKS * N_HALVES) as operands,
+        tc.tile_pool(name="results", bufs=N_BLOCKS * N_HALVES) as results,
         tc.tile_pool(name="residuals", bufs=2 * N_BLOCKS * N_HALVES) as residuals,
-        tc.tile_pool(name="passing", bufs=4) as passing,
         tc.psum_pool(name="banks", bufs=8) as banks,
     ):
         table_rows = held.tile([P, NODES // P, D_IN], BF16, name="table_rows")
@@ -54,7 +67,10 @@ def tile_gresnet_b_kernel(tc, table, w_self0, w_neigh0, b0, w_hid, b_hid, offs, 
 
         def round_weights(l):
             for kb in range(N_BLOCKS):
-                nc.vector.tensor_copy(w_bf16[l][:, kb, :], w_f32[l][:, kb, :])
+                if l % 2 == 0:
+                    nc.vector.tensor_copy(w_bf16[l][:, kb, :], w_f32[l][:, kb, :])
+                else:
+                    nc.vector.tensor_scalar(w_bf16[l][:, kb, :], w_f32[l][:, kb, :], 0.5, None, MULT)
 
         identity = held.tile([P, P], BF16, name="identity")
         make_identity(nc, identity[:])
@@ -79,7 +95,20 @@ def tile_gresnet_b_kernel(tc, table, w_self0, w_neigh0, b0, w_hid, b_hid, offs, 
                     start=True,
                     stop=False,
                 )
-        x_f32, x_bf16 = {}, {}
+        bias_halved = held.tile([P, N_BLOCKS, LAYERS], F32, name="bias_halved")
+        nc.vector.tensor_scalar(bias_halved[:], bias_hid[:], 0.5, None, MULT)
+        bias_halved_neg = held.tile([P, N_BLOCKS, LAYERS], F32, name="bias_halved_neg")
+        nc.vector.tensor_scalar(bias_halved_neg[:], bias_hid[:], -0.5, None, MULT)
+
+        carried = {}
+
+        def carry(t, mb, h, l):
+            carried[mb, h] = residuals.tile([P, HALF], F32, tag="carried", name=f"carried_{mb}_{h}")
+            nc.scalar.activation(
+                carried[mb, h][:], t[:], IDENTITY, bias=bias_halved[:, mb, l:l + 1], scale=0.5
+            )
+
+        x_bf16 = {}
         for h in range(N_HALVES):
             for mb in range(N_BLOCKS):
                 for e in range(DEGREE):
@@ -94,28 +123,27 @@ def tile_gresnet_b_kernel(tc, table, w_self0, w_neigh0, b0, w_hid, b_hid, offs, 
                         start=False,
                         stop=(e == DEGREE - 1),
                     )
-                x_f32[mb, h] = residuals.tile([P, HALF], F32, tag="x_f32", name=f"x_f32_{mb}_{h}")
-                nc.scalar.activation(
-                    x_f32[mb, h][:], acc_first[mb, h][:], RELU, bias=bias_first[:, mb:mb + 1]
-                )
+                x_f32 = results.tile([P, HALF], F32, tag="x_f32", name="x_f32")
+                nc.scalar.activation(x_f32[:], acc_first[mb, h][:], RELU, bias=bias_first[:, mb:mb + 1])
                 x_bf16[mb, h] = operands.tile([P, HALF], BF16, tag="x_bf16", name=f"x_bf16_{mb}_{h}")
-                nc.vector.tensor_copy(x_bf16[mb, h][:], x_f32[mb, h][:])
+                nc.vector.tensor_copy(x_bf16[mb, h][:], x_f32[:])
+                carry(x_f32, mb, h, 1)
 
-        bias_halved = held.tile([P, N_BLOCKS, LAYERS], F32, name="bias_halved")
-        nc.vector.tensor_scalar(bias_halved[:], bias_hid[:], 0.5, None, MULT)
         for l in range(LAYERS):
             closes_block = l % 2 == 1
             if l + 1 < LAYERS:
                 round_weights(l + 1)
             y_bf16 = {}
-            for h in range(N_HALVES):
+            for first, width in runs_of_nodes(l):
+                h = first // HALF
+                cols = slice(first - h * HALF, first - h * HALF + width)
                 for mb in range(N_BLOCKS):
-                    acc = banks.tile([P, HALF], F32, tag="bank", name="acc")
+                    acc = banks.tile([P, width], F32, tag="bank", name="acc")
                     for kb in range(N_BLOCKS):
                         nc.tensor.matmul(
                             acc[:],
                             w_bf16[l][:, kb, mb * P:(mb + 1) * P],
-                            x_bf16[kb, h][:],
+                            x_bf16[kb, h][:, cols],
                             start=(kb == 0),
                             stop=(kb == N_BLOCKS - 1),
                         )
@@ -131,19 +159,13 @@ def tile_gresnet_b_kernel(tc, table, w_self0, w_neigh0, b0, w_hid, b_hid, offs, 
                                 y_bf16[mb, h][:], acc[:], bias_hid[:, mb, l:l + 1], 0.0, ADD, MAX
                             )
                     else:
-                        half_relu = passing.tile([P, HALF], F32, tag="half_relu", name="half_relu")
-                        nc.scalar.activation(
-                            half_relu[:], acc[:], RELU, bias=bias_halved[:, mb, l:l + 1], scale=0.5
-                        )
-                        t = x_f32[mb, h]
-                        x_f32[mb, h] = residuals.tile([P, HALF], F32, tag="x_f32", name=f"x_f32_{mb}_{h}")
+                        x_f32 = results.tile([P, width], F32, tag="x_f32", name="x_f32")
                         nc.vector.scalar_tensor_tensor(
-                            x_f32[mb, h][:], t[:], 0.5, half_relu[:], MULT, ADD
+                            x_f32[:], acc[:], bias_halved_neg[:, mb, l:l + 1], carried[mb, h][:, cols], MAX, ADD
                         )
                         if l + 1 < LAYERS:
-                            nc.vector.tensor_copy(y_bf16[mb, h][:], x_f32[mb, h][:])
+                            nc.vector.tensor_copy(y_bf16[mb, h][:], x_f32[:])
+                            carry(x_f32, mb, h, l + 2)
                         else:
-                            nc.sync.dma_start(
-                                out[mb * P:(mb + 1) * P, h * HALF:(h + 1) * HALF], x_f32[mb, h][:]
-                            )
+                            nc.sync.dma_start(out[mb * P:(mb + 1) * P, first:first + width], x_f32[:])
             x_bf16 = y_bf16

@@ -15,7 +15,9 @@ HALF = 512
 N_HALVES = NODES // HALF
 N_BLOCKS = D_HID // P
 PIECE_COLS = HALF // 16
-ROW_BLOCKS = HALF // P
+QUARTER = 256
+N_QUARTERS = NODES // QUARTER
+ROW_BLOCKS = QUARTER // P
 NARROWEST = 128
 
 FLOPS = 2 * NODES * D_HID * (2 * D_IN + LAYERS * D_HID)
@@ -44,9 +46,9 @@ def tile_gresnet_b_kernel(tc, table, w_self0, w_neigh0, b0, w_hid, b_hid, offs, 
     ):
         table_rows = held.tile([P, NODES // P, D_IN], BF16, name="table_rows")
         table_blocks = table.rearrange("(a p) k -> p a k", p=P)
-        for h in range(N_HALVES):
-            blocks_of_half = slice(h * ROW_BLOCKS, (h + 1) * ROW_BLOCKS)
-            nc.sync.dma_start(table_rows[:, blocks_of_half, :], table_blocks[:, blocks_of_half, :])
+        for q in range(N_QUARTERS):
+            blocks_of_quarter = slice(q * ROW_BLOCKS, (q + 1) * ROW_BLOCKS)
+            nc.sync.dma_start(table_rows[:, blocks_of_quarter, :], table_blocks[:, blocks_of_quarter, :])
         w_self = held.tile([D_IN, D_HID], BF16, name="w_self")
         nc.sync.dma_start(w_self[:], w_self0)
         w_neigh = held.tile([D_IN, D_HID], BF16, name="w_neigh")
@@ -56,31 +58,33 @@ def tile_gresnet_b_kernel(tc, table, w_self0, w_neigh0, b0, w_hid, b_hid, offs, 
         bias_first = held.tile([P, N_BLOCKS], F32, name="bias_first")
         with nc.allow_non_contiguous_dma(reason="512 biases, one value to a partition and block"):
             nc.sync.dma_start(bias_first[:], b0.rearrange("(a p) o -> p (a o)", p=P))
-        w_f32 = [held.tile([P, N_BLOCKS, D_HID], F32, name=f"w_f32_{l}") for l in range(LAYERS)]
         bias_hid = held.tile([P, N_BLOCKS, LAYERS], F32, name="bias_hid")
+        nc.sync.dma_start(bias_hid[:], b_hid.rearrange("(a p) l -> p a l", p=P))
+        w_f32 = [held.tile([P, N_BLOCKS, D_HID], F32, name=f"w_f32_{l}") for l in range(LAYERS)]
         for l in range(LAYERS):
             nc.sync.dma_start(w_f32[l][:], w_hid[l].rearrange("(a p) m -> p a m", p=P))
-            if l == 0:
-                nc.sync.dma_start(bias_hid[:], b_hid.rearrange("(a p) l -> p a l", p=P))
-
-        w_bf16 = [held.tile([P, N_BLOCKS, D_HID], BF16, name=f"w_bf16_{l}") for l in range(LAYERS)]
-
-        def round_weights(l):
-            for kb in range(N_BLOCKS):
-                if l % 2 == 0:
-                    nc.vector.tensor_copy(w_bf16[l][:, kb, :], w_f32[l][:, kb, :])
-                else:
-                    nc.vector.tensor_scalar(w_bf16[l][:, kb, :], w_f32[l][:, kb, :], 0.5, None, MULT)
 
         identity = held.tile([P, P], BF16, name="identity")
         make_identity(nc, identity[:])
         table_t = held.tile([D_IN, NODES], BF16, name="table_t")
-        for h in range(N_HALVES):
-            flipped = banks.tile([D_IN, HALF], BF16, tag="bank", name="flipped")
+        for q in range(N_QUARTERS):
+            flipped = banks.tile([D_IN, QUARTER], BF16, tag="bank", name="flipped")
             for j in range(ROW_BLOCKS):
-                a = h * ROW_BLOCKS + j
+                a = q * ROW_BLOCKS + j
                 nc.tensor.transpose(flipped[:, j * P:(j + 1) * P], table_rows[:, a, :], identity[:])
-            nc.scalar.copy(table_t[:, h * HALF:(h + 1) * HALF], flipped[:])
+            nc.vector.tensor_copy(table_t[:, q * QUARTER:(q + 1) * QUARTER], flipped[:])
+
+        bias_halved = held.tile([P, N_BLOCKS, LAYERS], F32, name="bias_halved")
+        nc.gpsimd.tensor_scalar(bias_halved[:], bias_hid[:], 0.5, None, MULT)
+        bias_halved_neg = held.tile([P, N_BLOCKS, LAYERS], F32, name="bias_halved_neg")
+        nc.gpsimd.tensor_scalar(bias_halved_neg[:], bias_hid[:], -0.5, None, MULT)
+
+        w_bf16 = [held.tile([P, N_BLOCKS, D_HID], BF16, name=f"w_bf16_{l}") for l in range(LAYERS)]
+
+        def round_weights(l):
+            factor = 1.0 if l % 2 == 0 else 0.5
+            for kb in range(N_BLOCKS):
+                nc.scalar.mul(w_bf16[l][:, kb, :], w_f32[l][:, kb, :], factor)
 
         round_weights(0)
 
@@ -95,10 +99,6 @@ def tile_gresnet_b_kernel(tc, table, w_self0, w_neigh0, b0, w_hid, b_hid, offs, 
                     start=True,
                     stop=False,
                 )
-        bias_halved = held.tile([P, N_BLOCKS, LAYERS], F32, name="bias_halved")
-        nc.vector.tensor_scalar(bias_halved[:], bias_hid[:], 0.5, None, MULT)
-        bias_halved_neg = held.tile([P, N_BLOCKS, LAYERS], F32, name="bias_halved_neg")
-        nc.vector.tensor_scalar(bias_halved_neg[:], bias_hid[:], -0.5, None, MULT)
 
         carried = {}
 
@@ -107,6 +107,12 @@ def tile_gresnet_b_kernel(tc, table, w_self0, w_neigh0, b0, w_hid, b_hid, offs, 
             nc.scalar.activation(
                 carried[mb, h][:], t[:], IDENTITY, bias=bias_halved[:, mb, l:l + 1], scale=0.5
             )
+
+        def relu_out_of_psum(x, acc, bias, mb):
+            if mb % 2 == 0:
+                nc.scalar.activation(x, acc, RELU, bias=bias)
+            else:
+                nc.vector.tensor_scalar(x, acc, bias, 0.0, ADD, MAX)
 
         x_bf16 = {}
         for h in range(N_HALVES):
@@ -124,7 +130,7 @@ def tile_gresnet_b_kernel(tc, table, w_self0, w_neigh0, b0, w_hid, b_hid, offs, 
                         stop=(e == DEGREE - 1),
                     )
                 x_f32 = results.tile([P, HALF], F32, tag="x_f32", name="x_f32")
-                nc.scalar.activation(x_f32[:], acc_first[mb, h][:], RELU, bias=bias_first[:, mb:mb + 1])
+                relu_out_of_psum(x_f32[:], acc_first[mb, h][:], bias_first[:, mb:mb + 1], mb)
                 x_bf16[mb, h] = operands.tile([P, HALF], BF16, tag="x_bf16", name=f"x_bf16_{mb}_{h}")
                 nc.vector.tensor_copy(x_bf16[mb, h][:], x_f32[:])
                 carry(x_f32, mb, h, 1)
@@ -150,14 +156,7 @@ def tile_gresnet_b_kernel(tc, table, w_self0, w_neigh0, b0, w_hid, b_hid, offs, 
                     if l + 1 < LAYERS:
                         y_bf16[mb, h] = operands.tile([P, HALF], BF16, tag="x_bf16", name=f"y_bf16_{mb}_{h}")
                     if not closes_block:
-                        if mb % 2 == 0:
-                            nc.scalar.activation(
-                                y_bf16[mb, h][:], acc[:], RELU, bias=bias_hid[:, mb, l:l + 1]
-                            )
-                        else:
-                            nc.vector.tensor_scalar(
-                                y_bf16[mb, h][:], acc[:], bias_hid[:, mb, l:l + 1], 0.0, ADD, MAX
-                            )
+                        relu_out_of_psum(y_bf16[mb, h][:], acc[:], bias_hid[:, mb, l:l + 1], mb)
                     else:
                         x_f32 = results.tile([P, width], F32, tag="x_f32", name="x_f32")
                         nc.vector.scalar_tensor_tensor(

@@ -65,7 +65,8 @@ def tile_gresnet_b_kernel(tc, table, w_self0, w_neigh0, b0, w_hid, b_hid, offs, 
             nc.sync.dma_start(w_f32[l][:], w_hid[l].rearrange("(a p) m -> p a m", p=P))
 
         identity = held.tile([P, P], BF16, name="identity")
-        make_identity(nc, identity[:])
+        nc.vector.memset(identity[:], 0.0)
+        make_identity(nc, identity[:], nomemset=True)
         table_t = held.tile([D_IN, NODES], BF16, name="table_t")
         for q in range(N_QUARTERS):
             flipped = banks.tile([D_IN, QUARTER], BF16, tag="bank", name="flipped")

@@ -18,6 +18,7 @@ PIECE_COLS = HALF // 16
 QUARTER = 256
 N_QUARTERS = NODES // QUARTER
 ROW_BLOCKS = QUARTER // P
+QUARTERS_IN_HALF = HALF // QUARTER
 NARROWEST = 128
 
 FLOPS = 2 * NODES * D_HID * (2 * D_IN + LAYERS * D_HID)
@@ -46,11 +47,12 @@ def tile_gresnet_b_kernel(tc, table, w_self0, w_neigh0, b0, w_hid, b_hid, offs, 
     ):
         table_rows = held.tile([P, NODES // P, D_IN], BF16, name="table_rows")
         table_blocks = table.rearrange("(a p) k -> p a k", p=P)
+        w_self = held.tile([D_IN, D_HID], BF16, name="w_self")
         for q in range(N_QUARTERS):
             blocks_of_quarter = slice(q * ROW_BLOCKS, (q + 1) * ROW_BLOCKS)
             nc.sync.dma_start(table_rows[:, blocks_of_quarter, :], table_blocks[:, blocks_of_quarter, :])
-        w_self = held.tile([D_IN, D_HID], BF16, name="w_self")
-        nc.sync.dma_start(w_self[:], w_self0)
+            if q == 0:
+                nc.sync.dma_start(w_self[:], w_self0)
         w_neigh = held.tile([D_IN, D_HID], BF16, name="w_neigh")
         nc.sync.dma_start(w_neigh[:], w_neigh0)
         offsets = held.tile([P, DEGREE * NODES // 16], U16, name="offsets")
@@ -68,12 +70,34 @@ def tile_gresnet_b_kernel(tc, table, w_self0, w_neigh0, b0, w_hid, b_hid, offs, 
         nc.vector.memset(identity[:], 0.0)
         make_identity(nc, identity[:], nomemset=True)
         table_t = held.tile([D_IN, NODES], BF16, name="table_t")
-        for q in range(N_QUARTERS):
+
+        def flip_quarter(q):
             flipped = banks.tile([D_IN, QUARTER], BF16, tag="bank", name="flipped")
             for j in range(ROW_BLOCKS):
                 a = q * ROW_BLOCKS + j
                 nc.tensor.transpose(flipped[:, j * P:(j + 1) * P], table_rows[:, a, :], identity[:])
             nc.vector.tensor_copy(table_t[:, q * QUARTER:(q + 1) * QUARTER], flipped[:])
+
+        acc_first = {}
+
+        def project_own_nodes(q):
+            h, part = divmod(q, QUARTERS_IN_HALF)
+            for mb in range(N_BLOCKS):
+                if part == 0:
+                    acc_first[mb, h] = banks.tile([P, HALF], F32, tag="bank", name=f"acc_first_{mb}_{h}")
+                nc.tensor.matmul(
+                    acc_first[mb, h][:, part * QUARTER:(part + 1) * QUARTER],
+                    w_self[:, mb * P:(mb + 1) * P],
+                    table_t[:, q * QUARTER:(q + 1) * QUARTER],
+                    start=(part == 0),
+                    stop=False,
+                )
+
+        flip_quarter(0)
+        for q in range(N_QUARTERS):
+            if q + 1 < N_QUARTERS:
+                flip_quarter(q + 1)
+            project_own_nodes(q)
 
         bias_halved = held.tile([P, N_BLOCKS, LAYERS], F32, name="bias_halved")
         nc.gpsimd.tensor_scalar(bias_halved[:], bias_hid[:], 0.5, None, MULT)
@@ -88,18 +112,6 @@ def tile_gresnet_b_kernel(tc, table, w_self0, w_neigh0, b0, w_hid, b_hid, offs, 
                 nc.scalar.mul(w_bf16[l][:, kb, :], w_f32[l][:, kb, :], factor)
 
         round_weights(0)
-
-        acc_first = {}
-        for h in range(N_HALVES):
-            for mb in range(N_BLOCKS):
-                acc_first[mb, h] = banks.tile([P, HALF], F32, tag="bank", name=f"acc_first_{mb}_{h}")
-                nc.tensor.matmul(
-                    acc_first[mb, h][:],
-                    w_self[:, mb * P:(mb + 1) * P],
-                    table_t[:, h * HALF:(h + 1) * HALF],
-                    start=True,
-                    stop=False,
-                )
 
         carried = {}
 

@@ -41,7 +41,7 @@ def tile_gresnet_b_kernel(tc, table, w_self0, w_neigh0, b0, w_hid, b_hid, offs, 
     with (
         tc.tile_pool(name="held", bufs=1) as held,
         tc.tile_pool(name="operands", bufs=2 * N_BLOCKS * N_HALVES) as operands,
-        tc.tile_pool(name="results", bufs=N_BLOCKS * N_HALVES) as results,
+        tc.tile_pool(name="results", bufs=N_BLOCKS * len(runs_of_nodes(LAYERS - 1))) as results,
         tc.tile_pool(name="residuals", bufs=2 * N_BLOCKS * N_HALVES) as residuals,
         tc.psum_pool(name="banks", bufs=8) as banks,
     ):

@@ -15,10 +15,8 @@ HALF = 512
 N_HALVES = NODES // HALF
 N_BLOCKS = D_HID // P
 PIECE_COLS = HALF // 16
-QUARTER = 256
-N_QUARTERS = NODES // QUARTER
-ROW_BLOCKS = QUARTER // P
-QUARTERS_IN_HALF = HALF // QUARTER
+N_SLABS = NODES // P
+SLABS_IN_HALF = HALF // P
 NARROWEST = 128
 
 FLOPS = 2 * NODES * D_HID * (2 * D_IN + LAYERS * D_HID)
@@ -45,13 +43,11 @@ def tile_gresnet_b_kernel(tc, table, w_self0, w_neigh0, b0, w_hid, b_hid, offs, 
         tc.tile_pool(name="residuals", bufs=2 * N_BLOCKS * N_HALVES) as residuals,
         tc.psum_pool(name="banks", bufs=8) as banks,
     ):
-        table_rows = held.tile([P, NODES // P, D_IN], BF16, name="table_rows")
-        table_blocks = table.rearrange("(a p) k -> p a k", p=P)
+        table_rows = held.tile([P, N_SLABS, D_IN], BF16, name="table_rows")
         w_self = held.tile([D_IN, D_HID], BF16, name="w_self")
-        for q in range(N_QUARTERS):
-            blocks_of_quarter = slice(q * ROW_BLOCKS, (q + 1) * ROW_BLOCKS)
-            nc.sync.dma_start(table_rows[:, blocks_of_quarter, :], table_blocks[:, blocks_of_quarter, :])
-            if q == 0:
+        for s in range(N_SLABS):
+            nc.sync.dma_start(table_rows[:, s, :], table[s * P:(s + 1) * P, :])
+            if s == 0:
                 nc.sync.dma_start(w_self[:], w_self0)
         w_neigh = held.tile([D_IN, D_HID], BF16, name="w_neigh")
         nc.sync.dma_start(w_neigh[:], w_neigh0)
@@ -71,33 +67,33 @@ def tile_gresnet_b_kernel(tc, table, w_self0, w_neigh0, b0, w_hid, b_hid, offs, 
         make_identity(nc, identity[:], nomemset=True)
         table_t = held.tile([D_IN, NODES], BF16, name="table_t")
 
-        def flip_quarter(q):
-            flipped = banks.tile([D_IN, QUARTER], BF16, tag="bank", name="flipped")
-            for j in range(ROW_BLOCKS):
-                a = q * ROW_BLOCKS + j
-                nc.tensor.transpose(flipped[:, j * P:(j + 1) * P], table_rows[:, a, :], identity[:])
-            nc.vector.tensor_copy(table_t[:, q * QUARTER:(q + 1) * QUARTER], flipped[:])
+        def flip_slab(s):
+            flipped = banks.tile([D_IN, P], BF16, tag="bank", name="flipped")
+            nc.tensor.transpose(flipped[:], table_rows[:, s, :], identity[:])
+            nc.vector.tensor_copy(table_t[:, s * P:(s + 1) * P], flipped[:])
 
         acc_first = {}
 
-        def project_own_nodes(q):
-            h, part = divmod(q, QUARTERS_IN_HALF)
+        def project_own_nodes(s):
+            h, part = divmod(s, SLABS_IN_HALF)
             for mb in range(N_BLOCKS):
                 if part == 0:
                     acc_first[mb, h] = banks.tile([P, HALF], F32, tag="bank", name=f"acc_first_{mb}_{h}")
                 nc.tensor.matmul(
-                    acc_first[mb, h][:, part * QUARTER:(part + 1) * QUARTER],
+                    acc_first[mb, h][:, part * P:(part + 1) * P],
                     w_self[:, mb * P:(mb + 1) * P],
-                    table_t[:, q * QUARTER:(q + 1) * QUARTER],
+                    table_t[:, s * P:(s + 1) * P],
                     start=(part == 0),
                     stop=False,
                 )
 
-        flip_quarter(0)
-        for q in range(N_QUARTERS):
-            if q + 1 < N_QUARTERS:
-                flip_quarter(q + 1)
-            project_own_nodes(q)
+        flip_slab(0)
+        flip_slab(1)
+        for s in range(N_SLABS):
+            project_own_nodes(s)
+            for ahead in (2 * s + 2, 2 * s + 3):
+                if ahead < N_SLABS:
+                    flip_slab(ahead)
 
         bias_halved = held.tile([P, N_BLOCKS, LAYERS], F32, name="bias_halved")
         nc.gpsimd.tensor_scalar(bias_halved[:], bias_hid[:], 0.5, None, MULT)

import concourse.mybir as mybir
from concourse.masks import make_identity

BF16, F32, U16 = mybir.dt.bfloat16, mybir.dt.float32, mybir.dt.uint16
RELU, IDENTITY = mybir.ActivationFunctionType.Relu, mybir.ActivationFunctionType.Identity
ADD, MAX, MULT = mybir.AluOpType.add, mybir.AluOpType.max, mybir.AluOpType.mult

P = 128
NODES = 1024
D_IN = 128
D_HID = 512
DEGREE = 2
LAYERS = 6
HALF = 512
N_HALVES = NODES // HALF
N_BLOCKS = D_HID // P
PIECE_COLS = HALF // 16
N_SLABS = NODES // P
SLABS_IN_HALF = HALF // P
NARROWEST = 128

FLOPS = 2 * NODES * D_HID * (2 * D_IN + LAYERS * D_HID)


def runs_of_nodes(l):
    if l + 1 < LAYERS:
        return [(h * HALF, HALF) for h in range(N_HALVES)]
    runs, first = [(0, HALF)], HALF
    while NODES - first > NARROWEST:
        width = (NODES - first) // 2
        runs.append((first, width))
        first += width
    runs.append((first, NODES - first))
    return runs


def tile_gresnet_b_kernel(tc, table, w_self0, w_neigh0, b0, w_hid, b_hid, offs, out):
    nc = tc.nc
    with (
        tc.tile_pool(name="held", bufs=1) as held,
        tc.tile_pool(name="operands", bufs=2 * N_BLOCKS * N_HALVES) as operands,
        tc.tile_pool(name="results", bufs=N_BLOCKS * len(runs_of_nodes(LAYERS - 1))) as results,
        tc.tile_pool(name="residuals", bufs=2 * N_BLOCKS * N_HALVES) as residuals,
        tc.psum_pool(name="banks", bufs=8) as banks,
    ):
        table_rows = held.tile([P, N_SLABS, D_IN], BF16, name="table_rows")
        w_self = held.tile([D_IN, D_HID], BF16, name="w_self")
        for s in range(N_SLABS):
            nc.sync.dma_start(table_rows[:, s, :], table[s * P:(s + 1) * P, :])
            if s == 0:
                nc.sync.dma_start(w_self[:], w_self0)
        w_neigh = held.tile([D_IN, D_HID], BF16, name="w_neigh")
        nc.sync.dma_start(w_neigh[:], w_neigh0)
        offsets = held.tile([P, DEGREE * NODES // 16], U16, name="offsets")
        nc.sync.dma_start(offsets[:], offs)
        bias_first = held.tile([P, N_BLOCKS], F32, name="bias_first")
        with nc.allow_non_contiguous_dma(reason="512 biases, one value to a partition and block"):
            nc.sync.dma_start(bias_first[:], b0.rearrange("(a p) o -> p (a o)", p=P))
        bias_hid = held.tile([P, N_BLOCKS, LAYERS], F32, name="bias_hid")
        nc.sync.dma_start(bias_hid[:], b_hid.rearrange("(a p) l -> p a l", p=P))
        w_f32 = [held.tile([P, N_BLOCKS, D_HID], F32, name=f"w_f32_{l}") for l in range(LAYERS)]
        for l in range(LAYERS):
            nc.sync.dma_start(w_f32[l][:], w_hid[l].rearrange("(a p) m -> p a m", p=P))

        identity = held.tile([P, P], BF16, name="identity")
        nc.vector.memset(identity[:], 0.0)
        make_identity(nc, identity[:], nomemset=True)
        table_t = held.tile([D_IN, NODES], BF16, name="table_t")

        def flip_slab(s):
            flipped = banks.tile([D_IN, P], BF16, tag="bank", name="flipped")
            nc.tensor.transpose(flipped[:], table_rows[:, s, :], identity[:])
            nc.vector.tensor_copy(table_t[:, s * P:(s + 1) * P], flipped[:])

        acc_first = {}

        def project_own_nodes(s):
            h, part = divmod(s, SLABS_IN_HALF)
            for mb in range(N_BLOCKS):
                if part == 0:
                    acc_first[mb, h] = banks.tile([P, HALF], F32, tag="bank", name=f"acc_first_{mb}_{h}")
                nc.tensor.matmul(
                    acc_first[mb, h][:, part * P:(part + 1) * P],
                    w_self[:, mb * P:(mb + 1) * P],
                    table_t[:, s * P:(s + 1) * P],
                    start=(part == 0),
                    stop=False,
                )

        flip_slab(0)
        flip_slab(1)
        for s in range(N_SLABS):
            project_own_nodes(s)
            for ahead in (2 * s + 2, 2 * s + 3):
                if ahead < N_SLABS:
                    flip_slab(ahead)

        bias_halved = held.tile([P, N_BLOCKS, LAYERS], F32, name="bias_halved")
        nc.gpsimd.tensor_scalar(bias_halved[:], bias_hid[:], 0.5, None, MULT)
        bias_halved_neg = held.tile([P, N_BLOCKS, LAYERS], F32, name="bias_halved_neg")
        nc.gpsimd.tensor_scalar(bias_halved_neg[:], bias_hid[:], -0.5, None, MULT)

        w_bf16 = [held.tile([P, N_BLOCKS, D_HID], BF16, name=f"w_bf16_{l}") for l in range(LAYERS)]

        def round_weights(l):
            factor = 1.0 if l % 2 == 0 else 0.5
            for kb in range(N_BLOCKS):
                nc.scalar.mul(w_bf16[l][:, kb, :], w_f32[l][:, kb, :], factor)

        round_weights(0)

        carried = {}

        def carry(t, mb, h, l):
            carried[mb, h] = residuals.tile([P, HALF], F32, tag="carried", name=f"carried_{mb}_{h}")
            nc.scalar.activation(
                carried[mb, h][:], t[:], IDENTITY, bias=bias_halved[:, mb, l:l + 1], scale=0.5
            )

        def relu_out_of_psum(x, acc, bias, mb):
            if mb % 2 == 0:
                nc.scalar.activation(x, acc, RELU, bias=bias)
            else:
                nc.vector.tensor_scalar(x, acc, bias, 0.0, ADD, MAX)

        x_bf16 = {}
        for h in range(N_HALVES):
            for mb in range(N_BLOCKS):
                for e in range(DEGREE):
                    piece = e * N_HALVES + h
                    neighbours = table_t[:].indirect(
                        offsets[:, piece * PIECE_COLS:(piece + 1) * PIECE_COLS]
                    )
                    nc.tensor.matmul(
                        acc_first[mb, h][:],
                        w_neigh[:, mb * P:(mb + 1) * P],
                        neighbours,
                        start=False,
                        stop=(e == DEGREE - 1),
                    )
                x_f32 = results.tile([P, HALF], F32, tag="x_f32", name="x_f32")
                relu_out_of_psum(x_f32[:], acc_first[mb, h][:], bias_first[:, mb:mb + 1], mb)
                x_bf16[mb, h] = operands.tile([P, HALF], BF16, tag="x_bf16", name=f"x_bf16_{mb}_{h}")
                nc.vector.tensor_copy(x_bf16[mb, h][:], x_f32[:])
                carry(x_f32, mb, h, 1)

        for l in range(LAYERS):
            closes_block = l % 2 == 1
            if l + 1 < LAYERS:
                round_weights(l + 1)
            y_bf16 = {}
            for first, width in runs_of_nodes(l):
                h = first // HALF
                cols = slice(first - h * HALF, first - h * HALF + width)
                for mb in range(N_BLOCKS):
                    acc = banks.tile([P, width], F32, tag="bank", name="acc")
                    for kb in range(N_BLOCKS):
                        nc.tensor.matmul(
                            acc[:],
                            w_bf16[l][:, kb, mb * P:(mb + 1) * P],
                            x_bf16[kb, h][:, cols],
                            start=(kb == 0),
                            stop=(kb == N_BLOCKS - 1),
                        )
                    if l + 1 < LAYERS:
                        y_bf16[mb, h] = operands.tile([P, HALF], BF16, tag="x_bf16", name=f"y_bf16_{mb}_{h}")
                    if not closes_block:
                        relu_out_of_psum(y_bf16[mb, h][:], acc[:], bias_hid[:, mb, l:l + 1], mb)
                    else:
                        x_f32 = results.tile([P, width], F32, tag="x_f32", name="x_f32")
                        nc.vector.scalar_tensor_tensor(
                            x_f32[:], acc[:], bias_halved_neg[:, mb, l:l + 1], carried[mb, h][:, cols], MAX, ADD
                        )
                        if l + 1 < LAYERS:
                            nc.vector.tensor_copy(y_bf16[mb, h][:], x_f32[:])
                            carry(x_f32, mb, h, l + 2)
                        else:
                            nc.sync.dma_start(out[mb * P:(mb + 1) * P, first:first + width], x_f32[:])
            x_bf16 = y_bf16
